import numpy as np
import ml_dtypes


def mxq(x, axis, fmt="e4m3"):
    dtype, down = {"e4m3": (ml_dtypes.float8_e4m3fn, 7), "e5m2": (ml_dtypes.float8_e5m2, 14)}[fmt]
    v = np.moveaxis(np.asarray(x, np.float32).astype(ml_dtypes.bfloat16).astype(np.float64), axis, -1)
    blocks = v.reshape(v.shape[:-1] + (-1, 32))
    amax = np.abs(blocks).max(-1, keepdims=True)
    byte = np.maximum(np.where(amax > 0, np.frexp(amax)[1] - 1 + 127, 0) - down, 1)
    scale = np.exp2(byte - 127.0)
    codes = (blocks / scale).astype(np.float32).astype(dtype).astype(np.float64)
    return np.moveaxis((codes * scale).reshape(v.shape), -1, axis)


WIDE = False


def mx_kscale(k):
    if not WIDE:
        return np.ones(k)
    levels = np.array([10, -10, 5, -5, 0])
    a = np.random.permutation(np.resize(levels, k // 512 * 4)).reshape(k // 512, 4)
    idx = np.arange(k)
    return np.exp2(a[idx // 512, idx % 128 // 32])


BF16 = ml_dtypes.bfloat16


def bf(x):
    return np.asarray(x, np.float32).astype(BF16)


def f64(x):
    return np.asarray(x).astype(np.float64)


B, S, M, H, HKV, DH, R_T, R_H, R_W = 2, 2048, 1024, 2, 1, 128, 16, 24, 24
SECT = (2 * R_T, 2 * R_H, 2 * R_W)
NC = len(SECT)


def rotate_half(x):
    h = x.shape[-1] // 2
    return np.concatenate((-x[..., h:], x[..., :h]), axis=-1)


def mrope_combine(t):
    parts, off = [], 0
    for i, sz in enumerate(SECT):
        parts.append(t[i % NC, :, :, off:off + sz])
        off += sz
    return np.concatenate(parts, axis=-1)


def setup_inputs():
    s = mx_kscale(M)
    sd = 1.0 / np.sqrt(M)
    return {"hidden_states": bf(np.random.standard_normal((B, S, M)) * s),
            "cos": bf(np.random.standard_normal((NC, B, S, DH))),
            "sin": bf(np.random.standard_normal((NC, B, S, DH))),
            "Wq": bf(np.random.standard_normal((M, H, DH)) * sd / s[:, None, None]),
            "bq": bf(np.random.standard_normal((H, DH)) * 0.3),
            "Wk": bf(np.random.standard_normal((M, HKV, DH)) * sd / s[:, None, None]),
            "bk": bf(np.random.standard_normal((HKV, DH)) * 0.3),
            "Wv": bf(np.random.standard_normal((M, HKV, DH)) * sd / s[:, None, None]),
            "bv": bf(np.random.standard_normal((HKV, DH)) * 0.3)}


def reference(hidden_states, cos, sin, Wq, bq, Wk, bk, Wv, bv):
    xq = mxq(f64(hidden_states), 2, "e4m3")
    q = (xq @ mxq(f64(Wq).reshape(M, H * DH), 0, "e4m3")).reshape(B, S, H, DH) + f64(bq)
    k = (xq @ mxq(f64(Wk).reshape(M, HKV * DH), 0, "e4m3")).reshape(B, S, HKV, DH) + f64(bk)
    v = (xq @ mxq(f64(Wv).reshape(M, HKV * DH), 0, "e4m3")).reshape(B, S, HKV, DH) + f64(bv)
    cos_c = mrope_combine(f64(cos))[:, :, None, :]
    sin_c = mrope_combine(f64(sin))[:, :, None, :]
    q_rot = q * cos_c + rotate_half(q) * sin_c
    k_rot = k * cos_c + rotate_half(k) * sin_c
    return q_rot, k_rot, v

@@ -1,0 +1,307 @@
+from contextlib import ExitStack
+
+import concourse.mybir as mybir
+from concourse.masks import make_identity
+
+F32 = mybir.dt.float32
+BF16 = mybir.dt.bfloat16
+U32 = mybir.dt.uint32
+U8 = mybir.dt.uint8
+FP8X4 = mybir.dt.float8_e4m3fn_x4
+ALU = mybir.AluOpType
+ACT = mybir.ActivationFunctionType
+
+P = 128
+NB = 2
+TS = 16
+M = 1024
+NROUND = 16
+NGROUP = 8
+XBUFS = 5
+OBUFS = 4
+
+FLOPS = 2 * 4096 * 1024 * 512
+BYTES = 4096 * 1024 * 2 + 1024 * 512 * 2 + 2 * 4096 * 128 * 2 + 512 * 2 + 4096 * 512 * 4
+
+TABLE_BATCHES = ((0, 0, 4), (0, 4, 4), (0, 8, 8), (1, 0, 8), (1, 8, 8))
+
+
+def tile_qwen2vlattention_pa_t_kernel(
+    tc, hidden_states, cos, sin, Wq, bq, Wk, bk, Wv, bv, out_0, out_1, out_2
+):
+    nc = tc.nc
+    with ExitStack() as ctx:
+        ctx.enter_context(tc.manual_schedule())
+        const = ctx.enter_context(tc.tile_pool(name="const", bufs=1))
+        xpool = ctx.enter_context(tc.tile_pool(name="xpool", bufs=XBUFS))
+        rawp = ctx.enter_context(tc.tile_pool(name="rawp", bufs=2))
+        xgp = ctx.enter_context(tc.tile_pool(name="xgp", bufs=3))
+        xcp = ctx.enter_context(tc.tile_pool(name="xcp", bufs=4))
+        ytp = ctx.enter_context(tc.tile_pool(name="ytp", bufs=3))
+        ttp = ctx.enter_context(tc.tile_pool(name="ttp", bufs=2))
+        outp = ctx.enter_context(tc.tile_pool(name="outp", bufs=OBUFS))
+        psx = ctx.enter_context(tc.psum_pool(name="psx", bufs=2))
+        psm = ctx.enter_context(tc.psum_pool(name="psm", bufs=1))
+        psy = ctx.enter_context(tc.psum_pool(name="psy", bufs=4))
+
+        x_view = hidden_states.rearrange("b (p t) m -> b p t m", t=TS)
+        cos_view = cos.rearrange("c b (p t) d -> b p c t d", t=TS)
+        sin_view = sin.rearrange("c b (p t) d -> b p c t d", t=TS)
+        q_view = out_0.rearrange("b (p t) h d -> b p t (h d)", t=TS)
+        k_view = out_1.rearrange("b (p t) h d -> b p t (h d)", t=TS)
+        v_view = out_2.rearrange("b (p t) h d -> b p t (h d)", t=TS)
+
+        ident = const.tile([P, P], F32)
+        make_identity(nc, ident[:])
+
+        brow_bf = const.tile([P, P], BF16)
+        nc.vector.memset(brow_bf[:], 0.0)
+        nc.scalar.dma_start(out=brow_bf[0:2, :], in_=bq)
+        nc.scalar.dma_start(out=brow_bf[2:3, :], in_=bk)
+        bvb = const.tile([P, P], BF16)
+        nc.scalar.dma_start(out=bvb[:], in_=bv.rearrange("o d -> (o d)").partition_broadcast(P))
+
+        xin = {}
+        raws = {}
+
+        def load_x(grp, parts):
+            xt_in = xpool.tile([P, 4, M], BF16, name="xin")
+            xin[grp] = xt_in
+            b, t0 = grp // 4, 4 * (grp % 4)
+            step = 4 // parts
+            return [
+                (xt_in[:, i * step : (i + 1) * step, :], x_view[b, :, t0 + i * step : t0 + (i + 1) * step, :])
+                for i in range(parts)
+            ]
+
+        def load_table(k):
+            b, t0, tn = TABLE_BATCHES[k]
+            rawc = rawp.tile([P, 3, tn, P], BF16, name="rawc")
+            nc.sync.dma_start(out=rawc[:], in_=cos_view[b, :, :, t0 : t0 + tn, :])
+            rawsn = rawp.tile([P, 3, tn, P], BF16, name="rawsn")
+            nc.sync.dma_start(out=rawsn[:], in_=sin_view[b, :, :, t0 : t0 + tn, :])
+            raws[k] = (rawc, rawsn)
+
+        first = load_x(0, 2)
+        nc.sync.dma_start(out=first[0][0], in_=first[0][1])
+        wraw_q = const.tile([P, 4, 512], BF16)
+        nc.sync.dma_start(out=wraw_q[:], in_=Wq.rearrange("(a p e) h d -> p a (e h d)", a=4, e=2))
+        wraw_k = const.tile([P, 4, 256], BF16)
+        nc.sync.dma_start(out=wraw_k[:], in_=Wk.rearrange("(a p e) h d -> p a (e h d)", a=4, e=2))
+        wraw_v = const.tile([P, 4, 256], BF16)
+        nc.sync.dma_start(out=wraw_v[:], in_=Wv.rearrange("(a p e) h d -> p a (e h d)", a=4, e=2))
+        nc.sync.dma_start(out=first[1][0], in_=first[1][1])
+        for dst, src in load_x(1, 1):
+            nc.sync.dma_start(out=dst, in_=src)
+        load_table(0)
+        for dst, src in load_x(2, 1):
+            nc.sync.dma_start(out=dst, in_=src)
+        load_table(1)
+        for grp in (3, 4):
+            for dst, src in load_x(grp, 1):
+                nc.sync.dma_start(out=dst, in_=src)
+
+        wg = const.tile([P, 4, 2, P, 4], BF16, align_bytes=64)
+        wc = const.tile([P, 4, 2, P], U32, align_bytes=64)
+        ws = const.tile([P, 4, 2, P], U8, align_bytes=64)
+
+        def w_source(h):
+            if h < 2:
+                v5 = wraw_q[:].rearrange("p (g u) (e c) -> p g u e c", g=2, e=2)
+                return v5[:, :, :, :, h * P : (h + 1) * P]
+            raw = wraw_k if h == 2 else wraw_v
+            return raw[:].rearrange("p (g u) (e c) -> p g u e c", g=2, e=2)
+
+        def w_regroup(h, on_scalar):
+            src5 = w_source(h)
+            for g in range(2):
+                dst = wg[:, h, g].rearrange("p c (u e) -> p c u e", u=2)
+                src = src5[:, g].rearrange("p u e c -> p c u e")
+                if on_scalar:
+                    nc.scalar.copy(out=dst, in_=src)
+                else:
+                    nc.vector.tensor_copy(out=dst, in_=src)
+
+        def w_quantise(h):
+            nc.vector.quantize_mx(
+                out=wc[:, h].rearrange("p g c -> p (g c)").bitcast(FP8X4),
+                scales=ws[:, h].rearrange("p g c -> p (g c)"),
+                in_=wg[:, h].rearrange("p g c t -> p (g c t)"),
+            )
+
+        cs_of = {}
+
+        def combine(k):
+            b, t0, tn = TABLE_BATCHES[k]
+            rawc, rawsn = raws[k]
+            cst = const.tile([P, tn, 2, P], BF16, name="cs%d" % k)
+            for i in range(tn):
+                cs_of[(b, t0 + i)] = (cst, i)
+            nc.scalar.copy(out=cst[:, :, 0, 0:32], in_=rawc[:, 0, :, 0:32])
+            nc.scalar.copy(out=cst[:, :, 0, 32:80], in_=rawc[:, 1, :, 32:80])
+            nc.scalar.copy(out=cst[:, :, 0, 80:128], in_=rawc[:, 2, :, 80:128])
+            for lo, hi, comp, s0 in ((0, 16, 1, 64), (16, 64, 2, 80), (64, 96, 0, 0), (96, 128, 1, 32)):
+                nc.gpsimd.tensor_scalar(
+                    out=cst[:, :, 1, lo:hi],
+                    in0=rawsn[:, comp, :, s0 : s0 + hi - lo],
+                    scalar1=1.0,
+                    scalar2=0.0,
+                    op0=ALU.mult,
+                    op1=ALU.add,
+                )
+
+        xg_of, xc_of, yt_of, yb_of, tt_of, o_of = {}, {}, {}, {}, {}, {}
+        bias_col = const.tile([P, 4], F32)
+
+        def stage_a(r):
+            xt_in = xin[r // 2]
+            xg = xgp.tile([P, 1024], F32, align_bytes=64)
+            xg_of[r] = xg
+            for j in range(2):
+                words = xt_in[:, 2 * (r % 2) + j, :].bitcast(F32)
+                xt = psx.tile([P, 512], F32)
+                for i in range(4):
+                    nc.tensor.transpose(xt[:, i * P : (i + 1) * P], words[:, i * P : (i + 1) * P], ident[:])
+                nc.scalar.copy(
+                    out=xg[:].rearrange("p (g r u) -> p g r u", g=2, u=2)[:, :, j * P : (j + 1) * P, :],
+                    in_=xt[:].rearrange("p (g u r) -> p g r u", g=2, u=2),
+                )
+
+        def stage_q(r):
+            xc = xcp.tile([P, 512], U32, align_bytes=64)
+            xs = xcp.tile([P, 512], U8, align_bytes=64)
+            xc_of[r] = (xc, xs)
+            nc.vector.quantize_mx(out=xc[:].bitcast(FP8X4), scales=xs[:], in_=xg_of[r][:].bitcast(BF16))
+
+        def stage_b(r):
+            xc, xs = xc_of[r]
+            m0 = psm.tile([P, 2, 256], F32)
+            m1 = psm.tile([P, 256], F32)
+            yt = ytp.tile([P, 3, 256], F32)
+            yt_of[r] = yt
+            for h in range(3):
+                acc = m0[:, h, :] if h < 2 else m1[:]
+                for g in range(2):
+                    nc.tensor.matmul_mx(
+                        out=acc,
+                        lhsT=wc[:, h, g, :].bitcast(FP8X4),
+                        lhsT_scale=ws[:, h, g, :],
+                        rhs=xc[:, g * 256 : (g + 1) * 256].bitcast(FP8X4),
+                        rhs_scale=xs[:, g * 256 : (g + 1) * 256],
+                        start=(g == 0),
+                        stop=(g == 1),
+                    )
+            for h in range(3):
+                acc = m0[:, h, :] if h < 2 else m1[:]
+                nc.scalar.activation(
+                    out=yt[:, h, :], in_=acc, func=ACT.Identity, bias=bias_col[:, h : h + 1], scale=1.0
+                )
+
+        def stage_d(r):
+            xc, xs = xc_of[r]
+            yt = yt_of[r]
+            ybs = []
+            for j in range(2):
+                yb = psy.tile([P, 512], F32)
+                ybs.append(yb)
+                for g in range(2):
+                    c0 = g * 256 + j * P
+                    nc.tensor.matmul_mx(
+                        out=yb[:, 384:512],
+                        lhsT=xc[:, c0 : c0 + P].bitcast(FP8X4),
+                        lhsT_scale=xs[:, c0 : c0 + P],
+                        rhs=wc[:, 3, g, :].bitcast(FP8X4),
+                        rhs_scale=ws[:, 3, g, :],
+                        start=(g == 0),
+                        stop=(g == 1),
+                    )
+            for j in range(2):
+                for h in range(3):
+                    nc.tensor.transpose(
+                        ybs[j][:, h * P : (h + 1) * P], yt[:, h, j * P : (j + 1) * P], ident[:]
+                    )
+            yb_of[r] = ybs
+
+        def stage_e(r):
+            grp = r // 2
+            if r % 2 == 0:
+                tt = ttp.tile([P, 4, 2, 3, P], F32)
+                ov = outp.tile([P, 4, P], F32)
+                tt_of[grp] = tt
+                o_of[grp] = ov
+            tt = tt_of[grp]
+            ov = o_of[grp]
+            b = grp // 4
+            for j in range(2):
+                t4 = 2 * (r % 2) + j
+                cst, ci = cs_of[(b, 4 * (grp % 4) + t4)]
+                yb = yb_of[r][j]
+                nc.vector.tensor_tensor(
+                    out=tt[:, t4],
+                    in0=yb[:, 0:384].rearrange("p (h d) -> p h d", h=3).unsqueeze(1).to_broadcast([P, 2, 3, P]),
+                    in1=cst[:, ci].unsqueeze(2).to_broadcast([P, 2, 3, P]),
+                    op=ALU.mult,
+                )
+                nc.vector.tensor_tensor(out=ov[:, t4, :], in0=yb[:, 384:512], in1=bvb[:], op=ALU.add)
+
+        def stage_f(grp):
+            tt = tt_of[grp]
+            ov = o_of[grp]
+            b, t0 = grp // 4, 4 * (grp % 4)
+            oq = outp.tile([P, 4, 256], F32)
+            ok = outp.tile([P, 4, P], F32)
+            oq4 = oq[:].rearrange("p t (h d) -> p t h d", h=2)
+            nc.gpsimd.tensor_tensor(
+                out=oq4[:, :, :, 0:64], in0=tt[:, :, 0, 0:2, 0:64], in1=tt[:, :, 1, 0:2, 64:128], op=ALU.subtract
+            )
+            nc.gpsimd.tensor_tensor(
+                out=oq4[:, :, :, 64:128], in0=tt[:, :, 0, 0:2, 64:128], in1=tt[:, :, 1, 0:2, 0:64], op=ALU.add
+            )
+            nc.gpsimd.tensor_tensor(
+                out=ok[:, :, 0:64], in0=tt[:, :, 0, 2, 0:64], in1=tt[:, :, 1, 2, 64:128], op=ALU.subtract
+            )
+            nc.gpsimd.tensor_tensor(
+                out=ok[:, :, 64:128], in0=tt[:, :, 0, 2, 64:128], in1=tt[:, :, 1, 2, 0:64], op=ALU.add
+            )
+            nc.sync.dma_start(out=v_view[b, :, t0 : t0 + 4, :], in_=ov[:])
+            nc.sync.dma_start(out=q_view[b, :, t0 : t0 + 4, :], in_=oq[:])
+            nc.sync.dma_start(out=k_view[b, :, t0 : t0 + 4, :], in_=ok[:])
+
+        combine_at = {2: 0, 3: 1, 5: 2, 9: 3, 13: 4}
+
+        for s in range(NROUND + 3):
+            if s < NROUND:
+                stage_a(s)
+            if s == 0:
+                brow_f = const.tile([P, P], F32)
+                nc.vector.tensor_copy(out=brow_f[:], in_=brow_bf[:])
+                bt = psm.tile([P, 256], F32, name="m1")
+                nc.tensor.transpose(bt[:, 0:P], brow_f[:], ident[:])
+                nc.vector.tensor_copy(out=bias_col[:], in_=bt[:, 0:4])
+            if 0 <= s - 3:
+                stage_e(s - 3)
+                if (s - 3) % 2 == 1:
+                    stage_f((s - 3) // 2)
+            if s < NROUND:
+                stage_q(s)
+            if s == 0:
+                w_regroup(0, False)
+                w_regroup(1, True)
+                w_regroup(2, False)
+                w_quantise(0)
+                w_quantise(1)
+                w_regroup(3, False)
+                w_quantise(2)
+                w_quantise(3)
+            if 0 <= s - 1 < NROUND:
+                stage_b(s - 1)
+            if 0 <= s - 2 < NROUND:
+                stage_d(s - 2)
+            if s in combine_at:
+                k = combine_at[s]
+                combine(k)
+                if k + 2 < len(TABLE_BATCHES):
+                    load_table(k + 2)
+            if s % 2 == 1 and s // 2 + XBUFS < NGROUP:
+                for dst, src in load_x(s // 2 + XBUFS, 1):
+                    nc.sync.dma_start(out=dst, in_=src)

@@ -17,13 +17,14 @@ TS = 16
 M = 1024
 NROUND = 16
 NGROUP = 8
-XBUFS = 5
-OBUFS = 4
+XBUFS = 6
+OBUFS = 5
+RAWBUFS = 6
 
 FLOPS = 2 * 4096 * 1024 * 512
 BYTES = 4096 * 1024 * 2 + 1024 * 512 * 2 + 2 * 4096 * 128 * 2 + 512 * 2 + 4096 * 512 * 4
 
-TABLE_BATCHES = ((0, 0, 4), (0, 4, 4), (0, 8, 8), (1, 0, 8), (1, 8, 8))
+TABLE_BATCHES = ((0, 0, 4), (0, 4, 4), (0, 8, 4), (0, 12, 4), (1, 0, 4), (1, 4, 4), (1, 8, 4), (1, 12, 4))
 
 
 def tile_qwen2vlattention_pa_t_kernel(
@@ -34,7 +35,7 @@ def tile_qwen2vlattention_pa_t_kernel(
         ctx.enter_context(tc.manual_schedule())
         const = ctx.enter_context(tc.tile_pool(name="const", bufs=1))
         xpool = ctx.enter_context(tc.tile_pool(name="xpool", bufs=XBUFS))
-        rawp = ctx.enter_context(tc.tile_pool(name="rawp", bufs=2))
+        rawp = ctx.enter_context(tc.tile_pool(name="rawp", bufs=RAWBUFS))
         xgp = ctx.enter_context(tc.tile_pool(name="xgp", bufs=3))
         xcp = ctx.enter_context(tc.tile_pool(name="xcp", bufs=4))
         ytp = ctx.enter_context(tc.tile_pool(name="ytp", bufs=3))
@@ -56,10 +57,13 @@ def tile_qwen2vlattention_pa_t_kernel(
 
         brow_bf = const.tile([P, P], BF16)
         nc.vector.memset(brow_bf[:], 0.0)
+        warm = const.tile([P, 2], F32)
+        nc.vector.memset(warm[:], 0.0)
         nc.scalar.dma_start(out=brow_bf[0:2, :], in_=bq)
         nc.scalar.dma_start(out=brow_bf[2:3, :], in_=bk)
         bvb = const.tile([P, P], BF16)
         nc.scalar.dma_start(out=bvb[:], in_=bv.rearrange("o d -> (o d)").partition_broadcast(P))
+        nc.scalar.activation(out=warm[:, 1:2], in_=warm[:, 0:1], func=ACT.Identity, bias=0.0, scale=1.0)
 
         xin = {}
         raws = {}
@@ -84,41 +88,43 @@ def tile_qwen2vlattention_pa_t_kernel(
 
         first = load_x(0, 2)
         nc.sync.dma_start(out=first[0][0], in_=first[0][1])
-        wraw_q = const.tile([P, 4, 512], BF16)
-        nc.sync.dma_start(out=wraw_q[:], in_=Wq.rearrange("(a p e) h d -> p a (e h d)", a=4, e=2))
-        wraw_k = const.tile([P, 4, 256], BF16)
-        nc.sync.dma_start(out=wraw_k[:], in_=Wk.rearrange("(a p e) h d -> p a (e h d)", a=4, e=2))
-        wraw_v = const.tile([P, 4, 256], BF16)
-        nc.sync.dma_start(out=wraw_v[:], in_=Wv.rearrange("(a p e) h d -> p a (e h d)", a=4, e=2))
+        wraw = ttp.tile([P, 4096], BF16, name="tt", align_bytes=64)
+        wraw_q = wraw[:, 0:2048].rearrange("p (a c) -> p a c", a=4)
+        wraw_k = wraw[:, 2048:3072].rearrange("p (a c) -> p a c", a=4)
+        wraw_v = wraw[:, 3072:4096].rearrange("p (a c) -> p a c", a=4)
+        nc.sync.dma_start(out=wraw_q, in_=Wq.rearrange("(a p e) h d -> p a (e h d)", a=4, e=2))
+        nc.sync.dma_start(out=wraw_k, in_=Wk.rearrange("(a p e) h d -> p a (e h d)", a=4, e=2))
+        nc.sync.dma_start(out=wraw_v, in_=Wv.rearrange("(a p e) h d -> p a (e h d)", a=4, e=2))
         nc.sync.dma_start(out=first[1][0], in_=first[1][1])
         for dst, src in load_x(1, 1):
             nc.sync.dma_start(out=dst, in_=src)
-        load_table(0)
-        for dst, src in load_x(2, 1):
-            nc.sync.dma_start(out=dst, in_=src)
-        load_table(1)
-        for grp in (3, 4):
+        for grp in (2, 3, 4, 5):
+            load_table(grp - 2)
             for dst, src in load_x(grp, 1):
                 nc.sync.dma_start(out=dst, in_=src)
+        load_table(4)
+        load_table(5)
 
-        wg = const.tile([P, 4, 2, P, 4], BF16, align_bytes=64)
+        wg = ttp.tile([P, 4, 2, P, 4], BF16, name="tt", align_bytes=64)
         wc = const.tile([P, 4, 2, P], U32, align_bytes=64)
         ws = const.tile([P, 4, 2, P], U8, align_bytes=64)
 
         def w_source(h):
             if h < 2:
-                v5 = wraw_q[:].rearrange("p (g u) (e c) -> p g u e c", g=2, e=2)
+                v5 = wraw_q.rearrange("p (g u) (e c) -> p g u e c", g=2, e=2)
                 return v5[:, :, :, :, h * P : (h + 1) * P]
             raw = wraw_k if h == 2 else wraw_v
-            return raw[:].rearrange("p (g u) (e c) -> p g u e c", g=2, e=2)
+            return raw.rearrange("p (g u) (e c) -> p g u e c", g=2, e=2)
 
-        def w_regroup(h, on_scalar):
+        def w_regroup(h, engine):
             src5 = w_source(h)
             for g in range(2):
                 dst = wg[:, h, g].rearrange("p c (u e) -> p c u e", u=2)
                 src = src5[:, g].rearrange("p u e c -> p c u e")
-                if on_scalar:
+                if engine == "scalar":
                     nc.scalar.copy(out=dst, in_=src)
+                elif engine == "gpsimd":
+                    nc.gpsimd.tensor_scalar(out=dst, in0=src, scalar1=1.0, scalar2=0.0, op0=ALU.mult, op1=ALU.add)
                 else:
                     nc.vector.tensor_copy(out=dst, in_=src)
 
@@ -131,26 +137,26 @@ def tile_qwen2vlattention_pa_t_kernel(
 
         cs_of = {}
 
-        def combine(k):
+        cs_tile = {}
+
+        def combine_cos(k):
             b, t0, tn = TABLE_BATCHES[k]
-            rawc, rawsn = raws[k]
+            rawc = raws[k][0]
             cst = const.tile([P, tn, 2, P], BF16, name="cs%d" % k)
+            cs_tile[k] = cst
             for i in range(tn):
                 cs_of[(b, t0 + i)] = (cst, i)
             nc.scalar.copy(out=cst[:, :, 0, 0:32], in_=rawc[:, 0, :, 0:32])
             nc.scalar.copy(out=cst[:, :, 0, 32:80], in_=rawc[:, 1, :, 32:80])
             nc.scalar.copy(out=cst[:, :, 0, 80:128], in_=rawc[:, 2, :, 80:128])
-            for lo, hi, comp, s0 in ((0, 16, 1, 64), (16, 64, 2, 80), (64, 96, 0, 0), (96, 128, 1, 32)):
-                nc.gpsimd.tensor_scalar(
-                    out=cst[:, :, 1, lo:hi],
-                    in0=rawsn[:, comp, :, s0 : s0 + hi - lo],
-                    scalar1=1.0,
-                    scalar2=0.0,
-                    op0=ALU.mult,
-                    op1=ALU.add,
-                )
 
-        xg_of, xc_of, yt_of, yb_of, tt_of, o_of = {}, {}, {}, {}, {}, {}
+        def combine_sin(k):
+            rawsn = raws[k][1]
+            cst = cs_tile[k]
+            for lo, hi, comp, s0 in ((0, 16, 1, 64), (16, 64, 2, 80), (64, 96, 0, 0), (96, 128, 1, 32)):
+                nc.scalar.copy(out=cst[:, :, 1, lo:hi], in_=rawsn[:, comp, :, s0 : s0 + hi - lo])
+
+        xg_of, xc_of, yt_of, yb_of, tt_of, o_of, oqk_of = {}, {}, {}, {}, {}, {}, {}
         bias_col = const.tile([P, 4], F32)
 
         def stage_a(r):
@@ -225,8 +231,11 @@ def tile_qwen2vlattention_pa_t_kernel(
         def stage_e(r):
             grp = r // 2
             if r % 2 == 0:
-                tt = ttp.tile([P, 4, 2, 3, P], F32)
+                tt = ttp.tile([P, 4, 2, 3, P], F32, align_bytes=64)
                 ov = outp.tile([P, 4, P], F32)
+                oq = outp.tile([P, 4, 256], F32)
+                ok = outp.tile([P, 4, P], F32)
+                oqk_of[grp] = (oq, ok)
                 tt_of[grp] = tt
                 o_of[grp] = ov
             tt = tt_of[grp]
@@ -244,32 +253,34 @@ def tile_qwen2vlattention_pa_t_kernel(
                 )
                 nc.vector.tensor_tensor(out=ov[:, t4, :], in0=yb[:, 384:512], in1=bvb[:], op=ALU.add)
 
-        def stage_f(grp):
+        def stage_f(grp, ta, tb, q_engine):
             tt = tt_of[grp]
-            ov = o_of[grp]
-            b, t0 = grp // 4, 4 * (grp % 4)
-            oq = outp.tile([P, 4, 256], F32)
-            ok = outp.tile([P, 4, P], F32)
+            oq, ok = oqk_of[grp]
             oq4 = oq[:].rearrange("p t (h d) -> p t h d", h=2)
-            nc.gpsimd.tensor_tensor(
-                out=oq4[:, :, :, 0:64], in0=tt[:, :, 0, 0:2, 0:64], in1=tt[:, :, 1, 0:2, 64:128], op=ALU.subtract
+            q_engine.tensor_tensor(
+                out=oq4[:, ta:tb, :, 0:64], in0=tt[:, ta:tb, 0, 0:2, 0:64], in1=tt[:, ta:tb, 1, 0:2, 64:128],
+                op=ALU.subtract,
             )
-            nc.gpsimd.tensor_tensor(
-                out=oq4[:, :, :, 64:128], in0=tt[:, :, 0, 0:2, 64:128], in1=tt[:, :, 1, 0:2, 0:64], op=ALU.add
+            q_engine.tensor_tensor(
+                out=oq4[:, ta:tb, :, 64:128], in0=tt[:, ta:tb, 0, 0:2, 64:128], in1=tt[:, ta:tb, 1, 0:2, 0:64],
+                op=ALU.add,
             )
-            nc.gpsimd.tensor_tensor(
-                out=ok[:, :, 0:64], in0=tt[:, :, 0, 2, 0:64], in1=tt[:, :, 1, 2, 64:128], op=ALU.subtract
+            q_engine.tensor_tensor(
+                out=ok[:, ta:tb, 0:64], in0=tt[:, ta:tb, 0, 2, 0:64], in1=tt[:, ta:tb, 1, 2, 64:128], op=ALU.subtract
             )
-            nc.gpsimd.tensor_tensor(
-                out=ok[:, :, 64:128], in0=tt[:, :, 0, 2, 64:128], in1=tt[:, :, 1, 2, 0:64], op=ALU.add
+            q_engine.tensor_tensor(
+                out=ok[:, ta:tb, 64:128], in0=tt[:, ta:tb, 0, 2, 64:128], in1=tt[:, ta:tb, 1, 2, 0:64], op=ALU.add
             )
-            nc.sync.dma_start(out=v_view[b, :, t0 : t0 + 4, :], in_=ov[:])
-            nc.sync.dma_start(out=q_view[b, :, t0 : t0 + 4, :], in_=oq[:])
-            nc.sync.dma_start(out=k_view[b, :, t0 : t0 + 4, :], in_=ok[:])
 
-        combine_at = {2: 0, 3: 1, 5: 2, 9: 3, 13: 4}
+        def stores(grp, ta, tb):
+            b, t0 = grp // 4, 4 * (grp % 4)
+            oq, ok = oqk_of[grp]
+            nc.sync.dma_start(out=v_view[b, :, t0 + ta : t0 + tb, :], in_=o_of[grp][:, ta:tb, :])
+            nc.sync.dma_start(out=q_view[b, :, t0 + ta : t0 + tb, :], in_=oq[:, ta:tb, :])
+            nc.sync.dma_start(out=k_view[b, :, t0 + ta : t0 + tb, :], in_=ok[:, ta:tb, :])
 
         for s in range(NROUND + 3):
+            pending = []
             if s < NROUND:
                 stage_a(s)
             if s == 0:
@@ -279,29 +290,39 @@ def tile_qwen2vlattention_pa_t_kernel(
                 nc.tensor.transpose(bt[:, 0:P], brow_f[:], ident[:])
                 nc.vector.tensor_copy(out=bias_col[:], in_=bt[:, 0:4])
             if 0 <= s - 3:
-                stage_e(s - 3)
-                if (s - 3) % 2 == 1:
-                    stage_f((s - 3) // 2)
+                r = s - 3
+                stage_e(r)
+                if r // 2 == NGROUP - 1:
+                    ta = 2 * (r % 2)
+                    stage_f(r // 2, ta, ta + 2, nc.vector if r % 2 == 1 else nc.gpsimd)
+                    pending.append((r // 2, ta, ta + 2))
+                elif r % 2 == 1:
+                    stage_f(r // 2, 0, 4, nc.gpsimd)
+                    pending.append((r // 2, 0, 4))
             if s < NROUND:
                 stage_q(s)
             if s == 0:
-                w_regroup(0, False)
-                w_regroup(1, True)
-                w_regroup(2, False)
-                w_quantise(0)
-                w_quantise(1)
-                w_regroup(3, False)
-                w_quantise(2)
-                w_quantise(3)
+                w_regroup(0, "vector")
+                w_regroup(1, "scalar")
+                w_regroup(3, "gpsimd")
+                w_regroup(2, "vector")
+                for h in range(4):
+                    w_quantise(h)
             if 0 <= s - 1 < NROUND:
                 stage_b(s - 1)
             if 0 <= s - 2 < NROUND:
                 stage_d(s - 2)
-            if s in combine_at:
-                k = combine_at[s]
-                combine(k)
-                if k + 2 < len(TABLE_BATCHES):
-                    load_table(k + 2)
+            if s == 2:
+                combine_cos(0)
+            if s % 2 == 1 and 1 <= (s - 1) // 2 < NGROUP:
+                combine_cos((s - 1) // 2)
+            if s % 2 == 0 and 0 <= (s - 2) // 2 < NGROUP:
+                k = (s - 2) // 2
+                combine_sin(k)
+                if k + RAWBUFS < NGROUP:
+                    load_table(k + RAWBUFS)
             if s % 2 == 1 and s // 2 + XBUFS < NGROUP:
                 for dst, src in load_x(s // 2 + XBUFS, 1):
                     nc.sync.dma_start(out=dst, in_=src)
+            for grp, ta, tb in pending:
+                stores(grp, ta, tb)

@@ -24,7 +24,7 @@ RAWBUFS = 6
 FLOPS = 2 * 4096 * 1024 * 512
 BYTES = 4096 * 1024 * 2 + 1024 * 512 * 2 + 2 * 4096 * 128 * 2 + 512 * 2 + 4096 * 512 * 4
 
-TABLE_BATCHES = ((0, 0, 4), (0, 4, 4), (0, 8, 4), (0, 12, 4), (1, 0, 4), (1, 4, 4), (1, 8, 4), (1, 12, 4))
+TABLE_BATCHES = ((0, 0, 2), (0, 2, 2), (0, 4, 4), (0, 8, 4), (0, 12, 4), (1, 0, 4), (1, 4, 4), (1, 8, 4), (1, 12, 4))
 
 
 def tile_qwen2vlattention_pa_t_kernel(
@@ -86,8 +86,11 @@ def tile_qwen2vlattention_pa_t_kernel(
             nc.sync.dma_start(out=rawsn[:], in_=sin_view[b, :, :, t0 : t0 + tn, :])
             raws[k] = (rawc, rawsn)
 
-        first = load_x(0, 2)
-        nc.sync.dma_start(out=first[0][0], in_=first[0][1])
+        def start(pair):
+            nc.sync.dma_start(out=pair[0], in_=pair[1])
+
+        halves = [load_x(grp, 2) for grp in range(3)]
+        start(halves[0][0])
         wraw = ttp.tile([P, 4096], BF16, name="tt", align_bytes=64)
         wraw_q = wraw[:, 0:2048].rearrange("p (a c) -> p a c", a=4)
         wraw_k = wraw[:, 2048:3072].rearrange("p (a c) -> p a c", a=4)
@@ -95,15 +98,17 @@ def tile_qwen2vlattention_pa_t_kernel(
         nc.sync.dma_start(out=wraw_q, in_=Wq.rearrange("(a p e) h d -> p a (e h d)", a=4, e=2))
         nc.sync.dma_start(out=wraw_k, in_=Wk.rearrange("(a p e) h d -> p a (e h d)", a=4, e=2))
         nc.sync.dma_start(out=wraw_v, in_=Wv.rearrange("(a p e) h d -> p a (e h d)", a=4, e=2))
-        nc.sync.dma_start(out=first[1][0], in_=first[1][1])
-        for dst, src in load_x(1, 1):
-            nc.sync.dma_start(out=dst, in_=src)
-        for grp in (2, 3, 4, 5):
-            load_table(grp - 2)
-            for dst, src in load_x(grp, 1):
-                nc.sync.dma_start(out=dst, in_=src)
-        load_table(4)
-        load_table(5)
+        start(halves[0][1])
+        load_table(0)
+        start(halves[1][0])
+        load_table(1)
+        start(halves[1][1])
+        load_table(2)
+        start(halves[2][0])
+        start(halves[2][1])
+        for grp in (3, 4, 5):
+            load_table(grp)
+            start(load_x(grp, 1)[0])
 
         wg = ttp.tile([P, 4, 2, P, 4], BF16, name="tt", align_bytes=64)
         wc = const.tile([P, 4, 2, P], U32, align_bytes=64)
@@ -137,24 +142,19 @@ def tile_qwen2vlattention_pa_t_kernel(
 
         cs_of = {}
 
-        cs_tile = {}
-
-        def combine_cos(k):
+        def combine(k, on_vector):
             b, t0, tn = TABLE_BATCHES[k]
-            rawc = raws[k][0]
+            rawc, rawsn = raws[k]
             cst = const.tile([P, tn, 2, P], BF16, name="cs%d" % k)
-            cs_tile[k] = cst
             for i in range(tn):
                 cs_of[(b, t0 + i)] = (cst, i)
-            nc.scalar.copy(out=cst[:, :, 0, 0:32], in_=rawc[:, 0, :, 0:32])
-            nc.scalar.copy(out=cst[:, :, 0, 32:80], in_=rawc[:, 1, :, 32:80])
-            nc.scalar.copy(out=cst[:, :, 0, 80:128], in_=rawc[:, 2, :, 80:128])
-
-        def combine_sin(k):
-            rawsn = raws[k][1]
-            cst = cs_tile[k]
-            for lo, hi, comp, s0 in ((0, 16, 1, 64), (16, 64, 2, 80), (64, 96, 0, 0), (96, 128, 1, 32)):
-                nc.scalar.copy(out=cst[:, :, 1, lo:hi], in_=rawsn[:, comp, :, s0 : s0 + hi - lo])
+            moves = [(0, raw_lo, raw_hi, rawc, comp, raw_lo) for raw_lo, raw_hi, comp in ((0, 32, 0), (32, 80, 1), (80, 128, 2))]
+            moves += [(1, lo, hi, rawsn, comp, s0) for lo, hi, comp, s0 in ((0, 16, 1, 64), (16, 64, 2, 80), (64, 96, 0, 0), (96, 128, 1, 32))]
+            for row, lo, hi, raw, comp, s0 in moves:
+                if on_vector:
+                    nc.vector.tensor_copy(out=cst[:, :, row, lo:hi], in_=raw[:, comp, :, s0 : s0 + hi - lo])
+                else:
+                    nc.scalar.copy(out=cst[:, :, row, lo:hi], in_=raw[:, comp, :, s0 : s0 + hi - lo])
 
         xg_of, xc_of, yt_of, yb_of, tt_of, o_of, oqk_of = {}, {}, {}, {}, {}, {}, {}
         bias_col = const.tile([P, 4], F32)
@@ -203,9 +203,8 @@ def tile_qwen2vlattention_pa_t_kernel(
                     out=yt[:, h, :], in_=acc, func=ACT.Identity, bias=bias_col[:, h : h + 1], scale=1.0
                 )
 
-        def stage_d(r):
+        def stage_bv(r):
             xc, xs = xc_of[r]
-            yt = yt_of[r]
             ybs = []
             for j in range(2):
                 yb = psy.tile([P, 512], F32)
@@ -221,12 +220,15 @@ def tile_qwen2vlattention_pa_t_kernel(
                         start=(g == 0),
                         stop=(g == 1),
                     )
+            yb_of[r] = ybs
+
+        def stage_dtr(r):
+            yt = yt_of[r]
             for j in range(2):
                 for h in range(3):
                     nc.tensor.transpose(
-                        ybs[j][:, h * P : (h + 1) * P], yt[:, h, j * P : (j + 1) * P], ident[:]
+                        yb_of[r][j][:, h * P : (h + 1) * P], yt[:, h, j * P : (j + 1) * P], ident[:]
                     )
-            yb_of[r] = ybs
 
         def stage_e(r):
             grp = r // 2
@@ -245,13 +247,13 @@ def tile_qwen2vlattention_pa_t_kernel(
                 t4 = 2 * (r % 2) + j
                 cst, ci = cs_of[(b, 4 * (grp % 4) + t4)]
                 yb = yb_of[r][j]
+                nc.vector.tensor_tensor(out=ov[:, t4, :], in0=yb[:, 384:512], in1=bvb[:], op=ALU.add)
                 nc.vector.tensor_tensor(
                     out=tt[:, t4],
                     in0=yb[:, 0:384].rearrange("p (h d) -> p h d", h=3).unsqueeze(1).to_broadcast([P, 2, 3, P]),
                     in1=cst[:, ci].unsqueeze(2).to_broadcast([P, 2, 3, P]),
                     op=ALU.mult,
                 )
-                nc.vector.tensor_tensor(out=ov[:, t4, :], in0=yb[:, 384:512], in1=bvb[:], op=ALU.add)
 
         def stage_f(grp, ta, tb, q_engine):
             tt = tt_of[grp]
@@ -279,50 +281,59 @@ def tile_qwen2vlattention_pa_t_kernel(
             nc.sync.dma_start(out=q_view[b, :, t0 + ta : t0 + tb, :], in_=oq[:, ta:tb, :])
             nc.sync.dma_start(out=k_view[b, :, t0 + ta : t0 + tb, :], in_=ok[:, ta:tb, :])
 
-        for s in range(NROUND + 3):
+        first_round = [(8 * b + t0 // 2) for b, t0, tn in TABLE_BATCHES]
+        n_batches = len(TABLE_BATCHES)
+        loaded = [RAWBUFS]
+
+        def combines(s, on_vector):
+            for k in range(n_batches):
+                if (k < 2) != on_vector:
+                    continue
+                if s == first_round[k] + (2 if k < 2 else 1):
+                    combine(k, on_vector)
+                    if loaded[0] < n_batches:
+                        load_table(loaded[0])
+                        loaded[0] += 1
+
+        for s in range(NROUND + 2):
             pending = []
+            if 2 <= s <= 2:
+                stage_dtr(s - 2)
             if s < NROUND:
                 stage_a(s)
+            if s > 2:
+                stage_dtr(s - 2)
             if s == 0:
                 brow_f = const.tile([P, P], F32)
                 nc.vector.tensor_copy(out=brow_f[:], in_=brow_bf[:])
                 bt = psm.tile([P, 256], F32, name="m1")
                 nc.tensor.transpose(bt[:, 0:P], brow_f[:], ident[:])
                 nc.vector.tensor_copy(out=bias_col[:], in_=bt[:, 0:4])
-            if 0 <= s - 3:
-                r = s - 3
+                w_regroup(0, "vector")
+                w_regroup(1, "scalar")
+                stage_q(0)
+                w_regroup(2, "vector")
+                w_regroup(3, "scalar")
+                for h in range(4):
+                    w_quantise(h)
+            combines(s, True)
+            if s >= 2:
+                r = s - 2
                 stage_e(r)
                 if r // 2 == NGROUP - 1:
                     ta = 2 * (r % 2)
-                    stage_f(r // 2, ta, ta + 2, nc.vector if r % 2 == 1 else nc.gpsimd)
+                    stage_f(r // 2, ta, ta + 2, nc.vector)
                     pending.append((r // 2, ta, ta + 2))
                 elif r % 2 == 1:
                     stage_f(r // 2, 0, 4, nc.gpsimd)
                     pending.append((r // 2, 0, 4))
-            if s < NROUND:
+            if 0 < s < NROUND:
                 stage_q(s)
-            if s == 0:
-                w_regroup(0, "vector")
-                w_regroup(1, "scalar")
-                w_regroup(3, "gpsimd")
-                w_regroup(2, "vector")
-                for h in range(4):
-                    w_quantise(h)
-            if 0 <= s - 1 < NROUND:
+            if 1 <= s <= NROUND:
                 stage_b(s - 1)
-            if 0 <= s - 2 < NROUND:
-                stage_d(s - 2)
-            if s == 2:
-                combine_cos(0)
-            if s % 2 == 1 and 1 <= (s - 1) // 2 < NGROUP:
-                combine_cos((s - 1) // 2)
-            if s % 2 == 0 and 0 <= (s - 2) // 2 < NGROUP:
-                k = (s - 2) // 2
-                combine_sin(k)
-                if k + RAWBUFS < NGROUP:
-                    load_table(k + RAWBUFS)
+                stage_bv(s - 1)
+            combines(s, False)
             if s % 2 == 1 and s // 2 + XBUFS < NGROUP:
-                for dst, src in load_x(s // 2 + XBUFS, 1):
-                    nc.sync.dma_start(out=dst, in_=src)
+                start(load_x(s // 2 + XBUFS, 1)[0])
             for grp, ta, tb in pending:
                 stores(grp, ta, tb)

@@ -18,13 +18,13 @@ M = 1024
 NROUND = 16
 NGROUP = 8
 XBUFS = 6
-OBUFS = 5
-RAWBUFS = 6
+OBUFS = 3
 
 FLOPS = 2 * 4096 * 1024 * 512
 BYTES = 4096 * 1024 * 2 + 1024 * 512 * 2 + 2 * 4096 * 128 * 2 + 512 * 2 + 4096 * 512 * 4
 
 TABLE_BATCHES = ((0, 0, 2), (0, 2, 2), (0, 4, 4), (0, 8, 4), (0, 12, 4), (1, 0, 4), (1, 4, 4), (1, 8, 4), (1, 12, 4))
+TABLE_LOADS = ((0, 0, 2), (0, 2, 2), (0, 4, 4), (0, 8, 4), (0, 12, 4), (1, 0, 8), (1, 8, 8))
 
 
 def tile_qwen2vlattention_pa_t_kernel(
@@ -35,7 +35,6 @@ def tile_qwen2vlattention_pa_t_kernel(
         ctx.enter_context(tc.manual_schedule())
         const = ctx.enter_context(tc.tile_pool(name="const", bufs=1))
         xpool = ctx.enter_context(tc.tile_pool(name="xpool", bufs=XBUFS))
-        rawp = ctx.enter_context(tc.tile_pool(name="rawp", bufs=RAWBUFS))
         xgp = ctx.enter_context(tc.tile_pool(name="xgp", bufs=3))
         xcp = ctx.enter_context(tc.tile_pool(name="xcp", bufs=4))
         ytp = ctx.enter_context(tc.tile_pool(name="ytp", bufs=3))
@@ -79,12 +78,13 @@ def tile_qwen2vlattention_pa_t_kernel(
             ]
 
         def load_table(k):
-            b, t0, tn = TABLE_BATCHES[k]
-            rawc = rawp.tile([P, 3, tn, P], BF16, name="rawc")
+            b, t0, tn = TABLE_LOADS[k]
+            rawc = const.tile([P, 3, tn, P], BF16, name="rawc%d" % k)
             nc.sync.dma_start(out=rawc[:], in_=cos_view[b, :, :, t0 : t0 + tn, :])
-            rawsn = rawp.tile([P, 3, tn, P], BF16, name="rawsn")
+            rawsn = const.tile([P, 3, tn, P], BF16, name="rawsn%d" % k)
             nc.sync.dma_start(out=rawsn[:], in_=sin_view[b, :, :, t0 : t0 + tn, :])
-            raws[k] = (rawc, rawsn)
+            for i in range(tn):
+                raws[(b, t0 + i)] = (rawc, rawsn, i)
 
         def start(pair):
             nc.sync.dma_start(out=pair[0], in_=pair[1])
@@ -144,7 +144,7 @@ def tile_qwen2vlattention_pa_t_kernel(
 
         def combine(k, on_vector):
             b, t0, tn = TABLE_BATCHES[k]
-            rawc, rawsn = raws[k]
+            rawc, rawsn, r0 = raws[(b, t0)]
             cst = const.tile([P, tn, 2, P], BF16, name="cs%d" % k)
             for i in range(tn):
                 cs_of[(b, t0 + i)] = (cst, i)
@@ -152,11 +152,11 @@ def tile_qwen2vlattention_pa_t_kernel(
             moves += [(1, lo, hi, rawsn, comp, s0) for lo, hi, comp, s0 in ((0, 16, 1, 64), (16, 64, 2, 80), (64, 96, 0, 0), (96, 128, 1, 32))]
             for row, lo, hi, raw, comp, s0 in moves:
                 if on_vector:
-                    nc.vector.tensor_copy(out=cst[:, :, row, lo:hi], in_=raw[:, comp, :, s0 : s0 + hi - lo])
+                    nc.vector.tensor_copy(out=cst[:, :, row, lo:hi], in_=raw[:, comp, r0 : r0 + tn, s0 : s0 + hi - lo])
                 else:
-                    nc.scalar.copy(out=cst[:, :, row, lo:hi], in_=raw[:, comp, :, s0 : s0 + hi - lo])
+                    nc.scalar.copy(out=cst[:, :, row, lo:hi], in_=raw[:, comp, r0 : r0 + tn, s0 : s0 + hi - lo])
 
-        xg_of, xc_of, yt_of, yb_of, tt_of, o_of, oqk_of = {}, {}, {}, {}, {}, {}, {}
+        xg_of, xc_of, yt_of, yb_of, tt_of, o_of = {}, {}, {}, {}, {}, {}
         bias_col = const.tile([P, 4], F32)
 
         def stage_a(r):
@@ -232,22 +232,22 @@ def tile_qwen2vlattention_pa_t_kernel(
 
         def stage_e(r):
             grp = r // 2
+            if r % 4 == 0:
+                ov = outp.tile([P, 8, P], F32)
+                oq = outp.tile([P, 8, 256], F32)
+                ok = outp.tile([P, 8, P], F32)
+                o_of[grp // 2] = (ov, oq, ok)
             if r % 2 == 0:
                 tt = ttp.tile([P, 4, 2, 3, P], F32, align_bytes=64)
-                ov = outp.tile([P, 4, P], F32)
-                oq = outp.tile([P, 4, 256], F32)
-                ok = outp.tile([P, 4, P], F32)
-                oqk_of[grp] = (oq, ok)
                 tt_of[grp] = tt
-                o_of[grp] = ov
             tt = tt_of[grp]
-            ov = o_of[grp]
+            ov = o_of[grp // 2][0]
             b = grp // 4
             for j in range(2):
                 t4 = 2 * (r % 2) + j
                 cst, ci = cs_of[(b, 4 * (grp % 4) + t4)]
                 yb = yb_of[r][j]
-                nc.vector.tensor_tensor(out=ov[:, t4, :], in0=yb[:, 384:512], in1=bvb[:], op=ALU.add)
+                nc.vector.tensor_tensor(out=ov[:, 4 * (grp % 2) + t4, :], in0=yb[:, 384:512], in1=bvb[:], op=ALU.add)
                 nc.vector.tensor_tensor(
                     out=tt[:, t4],
                     in0=yb[:, 0:384].rearrange("p (h d) -> p h d", h=3).unsqueeze(1).to_broadcast([P, 2, 3, P]),
@@ -257,8 +257,9 @@ def tile_qwen2vlattention_pa_t_kernel(
 
         def stage_f(grp, ta, tb, q_engine):
             tt = tt_of[grp]
-            oq, ok = oqk_of[grp]
-            oq4 = oq[:].rearrange("p t (h d) -> p t h d", h=2)
+            so = 4 * (grp % 2)
+            oq4 = o_of[grp // 2][1][:, so : so + 4, :].rearrange("p t (h d) -> p t h d", h=2)
+            ok = o_of[grp // 2][2][:, so : so + 4, :]
             q_engine.tensor_tensor(
                 out=oq4[:, ta:tb, :, 0:64], in0=tt[:, ta:tb, 0, 0:2, 0:64], in1=tt[:, ta:tb, 1, 0:2, 64:128],
                 op=ALU.subtract,
@@ -274,16 +275,15 @@ def tile_qwen2vlattention_pa_t_kernel(
                 out=ok[:, ta:tb, 64:128], in0=tt[:, ta:tb, 0, 2, 64:128], in1=tt[:, ta:tb, 1, 2, 0:64], op=ALU.add
             )
 
-        def stores(grp, ta, tb):
-            b, t0 = grp // 4, 4 * (grp % 4)
-            oq, ok = oqk_of[grp]
-            nc.sync.dma_start(out=v_view[b, :, t0 + ta : t0 + tb, :], in_=o_of[grp][:, ta:tb, :])
+        def stores(pair, ta, tb):
+            b, t0 = pair // 2, 8 * (pair % 2)
+            ov, oq, ok = o_of[pair]
+            nc.sync.dma_start(out=v_view[b, :, t0 + ta : t0 + tb, :], in_=ov[:, ta:tb, :])
             nc.sync.dma_start(out=q_view[b, :, t0 + ta : t0 + tb, :], in_=oq[:, ta:tb, :])
             nc.sync.dma_start(out=k_view[b, :, t0 + ta : t0 + tb, :], in_=ok[:, ta:tb, :])
 
         first_round = [(8 * b + t0 // 2) for b, t0, tn in TABLE_BATCHES]
         n_batches = len(TABLE_BATCHES)
-        loaded = [RAWBUFS]
 
         def combines(s, on_vector):
             for k in range(n_batches):
@@ -291,9 +291,6 @@ def tile_qwen2vlattention_pa_t_kernel(
                     continue
                 if s == first_round[k] + (2 if k < 2 else 1):
                     combine(k, on_vector)
-                    if loaded[0] < n_batches:
-                        load_table(loaded[0])
-                        loaded[0] += 1
 
         for s in range(NROUND + 2):
             pending = []
@@ -320,20 +317,26 @@ def tile_qwen2vlattention_pa_t_kernel(
             if s >= 2:
                 r = s - 2
                 stage_e(r)
-                if r // 2 == NGROUP - 1:
+                grp = r // 2
+                if grp == NGROUP - 1:
                     ta = 2 * (r % 2)
-                    stage_f(r // 2, ta, ta + 2, nc.vector)
-                    pending.append((r // 2, ta, ta + 2))
+                    stage_f(grp, ta, ta + 2, nc.vector)
+                    pending.append((grp // 2, 4 + ta, 4 + ta + 2))
                 elif r % 2 == 1:
-                    stage_f(r // 2, 0, 4, nc.gpsimd)
-                    pending.append((r // 2, 0, 4))
+                    stage_f(grp, 0, 4, nc.gpsimd)
+                    if grp == NGROUP - 2:
+                        pending.append((grp // 2, 0, 4))
+                    elif grp % 2 == 1:
+                        pending.append((grp // 2, 0, 8))
             if 0 < s < NROUND:
                 stage_q(s)
             if 1 <= s <= NROUND:
                 stage_b(s - 1)
                 stage_bv(s - 1)
             combines(s, False)
+            if s == 3:
+                load_table(6)
             if s % 2 == 1 and s // 2 + XBUFS < NGROUP:
                 start(load_x(s // 2 + XBUFS, 1)[0])
-            for grp, ta, tb in pending:
-                stores(grp, ta, tb)
+            for pair, ta, tb in pending:
+                stores(pair, ta, tb)

@@ -255,23 +255,27 @@ def tile_qwen2vlattention_pa_t_kernel(
                     op=ALU.mult,
                 )
 
-        def stage_f(grp, ta, tb, q_engine):
+        def add_q(grp, ta, tb, engine):
             tt = tt_of[grp]
             so = 4 * (grp % 2)
             oq4 = o_of[grp // 2][1][:, so : so + 4, :].rearrange("p t (h d) -> p t h d", h=2)
-            ok = o_of[grp // 2][2][:, so : so + 4, :]
-            q_engine.tensor_tensor(
+            engine.tensor_tensor(
                 out=oq4[:, ta:tb, :, 0:64], in0=tt[:, ta:tb, 0, 0:2, 0:64], in1=tt[:, ta:tb, 1, 0:2, 64:128],
                 op=ALU.subtract,
             )
-            q_engine.tensor_tensor(
+            engine.tensor_tensor(
                 out=oq4[:, ta:tb, :, 64:128], in0=tt[:, ta:tb, 0, 0:2, 64:128], in1=tt[:, ta:tb, 1, 0:2, 0:64],
                 op=ALU.add,
             )
-            q_engine.tensor_tensor(
+
+        def add_k(grp, ta, tb):
+            tt = tt_of[grp]
+            so = 4 * (grp % 2)
+            ok = o_of[grp // 2][2][:, so : so + 4, :]
+            nc.vector.tensor_tensor(
                 out=ok[:, ta:tb, 0:64], in0=tt[:, ta:tb, 0, 2, 0:64], in1=tt[:, ta:tb, 1, 2, 64:128], op=ALU.subtract
             )
-            q_engine.tensor_tensor(
+            nc.vector.tensor_tensor(
                 out=ok[:, ta:tb, 64:128], in0=tt[:, ta:tb, 0, 2, 64:128], in1=tt[:, ta:tb, 1, 2, 0:64], op=ALU.add
             )
 
@@ -318,18 +322,18 @@ def tile_qwen2vlattention_pa_t_kernel(
                 r = s - 2
                 stage_e(r)
                 grp = r // 2
+                ta = 2 * (r % 2)
+                add_q(grp, ta, ta + 2, nc.vector if r == NROUND - 1 else nc.gpsimd)
                 if grp == NGROUP - 1:
-                    ta = 2 * (r % 2)
-                    stage_f(grp, ta, ta + 2, nc.vector)
                     pending.append((grp // 2, 4 + ta, 4 + ta + 2))
-                elif r % 2 == 1:
-                    stage_f(grp, 0, 4, nc.gpsimd)
-                    if grp == NGROUP - 2:
-                        pending.append((grp // 2, 0, 4))
-                    elif grp % 2 == 1:
-                        pending.append((grp // 2, 0, 8))
+                elif r % 2 == 1 and grp == NGROUP - 2:
+                    pending.append((grp // 2, 0, 4))
+                elif r % 4 == 3:
+                    pending.append((grp // 2, 0, 8))
             if 0 < s < NROUND:
                 stage_q(s)
+            if s >= 2:
+                add_k((s - 2) // 2, 2 * (s % 2), 2 * (s % 2) + 2)
             if 1 <= s <= NROUND:
                 stage_b(s - 1)
                 stage_bv(s - 1)

@@ -168,6 +168,7 @@ def tile_qwen2vlattention_pa_t_kernel(
                 xt = psx.tile([P, 512], F32)
                 for i in range(4):
                     nc.tensor.transpose(xt[:, i * P : (i + 1) * P], words[:, i * P : (i + 1) * P], ident[:])
+                    nc.tensor.transpose(xt[:, i * P : (i + 1) * P], words[:, i * P : (i + 1) * P], ident[:])
                 nc.scalar.copy(
                     out=xg[:].rearrange("p (g r u) -> p g r u", g=2, u=2)[:, :, j * P : (j + 1) * P, :],
                     in_=xt[:].rearrange("p (g u r) -> p g r u", g=2, u=2),

from contextlib import ExitStack

import concourse.mybir as mybir
from concourse.masks import make_identity

F32 = mybir.dt.float32
BF16 = mybir.dt.bfloat16
U32 = mybir.dt.uint32
U8 = mybir.dt.uint8
FP8X4 = mybir.dt.float8_e4m3fn_x4
ALU = mybir.AluOpType
ACT = mybir.ActivationFunctionType

P = 128
NB = 2
TS = 16
M = 1024
NROUND = 16
NGROUP = 8
XBUFS = 6
OBUFS = 3

FLOPS = 2 * 4096 * 1024 * 512
BYTES = 4096 * 1024 * 2 + 1024 * 512 * 2 + 2 * 4096 * 128 * 2 + 512 * 2 + 4096 * 512 * 4

TABLE_BATCHES = ((0, 0, 2), (0, 2, 2), (0, 4, 4), (0, 8, 4), (0, 12, 4), (1, 0, 4), (1, 4, 4), (1, 8, 4), (1, 12, 4))
TABLE_LOADS = ((0, 0, 2), (0, 2, 2), (0, 4, 4), (0, 8, 4), (0, 12, 4), (1, 0, 8), (1, 8, 8))


def tile_qwen2vlattention_pa_t_kernel(
    tc, hidden_states, cos, sin, Wq, bq, Wk, bk, Wv, bv, out_0, out_1, out_2
):
    nc = tc.nc
    with ExitStack() as ctx:
        ctx.enter_context(tc.manual_schedule())
        const = ctx.enter_context(tc.tile_pool(name="const", bufs=1))
        xpool = ctx.enter_context(tc.tile_pool(name="xpool", bufs=XBUFS))
        xgp = ctx.enter_context(tc.tile_pool(name="xgp", bufs=3))
        xcp = ctx.enter_context(tc.tile_pool(name="xcp", bufs=4))
        ytp = ctx.enter_context(tc.tile_pool(name="ytp", bufs=3))
        ttp = ctx.enter_context(tc.tile_pool(name="ttp", bufs=2))
        outp = ctx.enter_context(tc.tile_pool(name="outp", bufs=OBUFS))
        psx = ctx.enter_context(tc.psum_pool(name="psx", bufs=2))
        psm = ctx.enter_context(tc.psum_pool(name="psm", bufs=1))
        psy = ctx.enter_context(tc.psum_pool(name="psy", bufs=4))

        x_view = hidden_states.rearrange("b (p t) m -> b p t m", t=TS)
        cos_view = cos.rearrange("c b (p t) d -> b p c t d", t=TS)
        sin_view = sin.rearrange("c b (p t) d -> b p c t d", t=TS)
        q_view = out_0.rearrange("b (p t) h d -> b p t (h d)", t=TS)
        k_view = out_1.rearrange("b (p t) h d -> b p t (h d)", t=TS)
        v_view = out_2.rearrange("b (p t) h d -> b p t (h d)", t=TS)

        ident = const.tile([P, P], F32)
        make_identity(nc, ident[:])

        brow_bf = const.tile([P, P], BF16)
        nc.vector.memset(brow_bf[:], 0.0)
        warm = const.tile([P, 2], F32)
        nc.vector.memset(warm[:], 0.0)
        nc.scalar.dma_start(out=brow_bf[0:2, :], in_=bq)
        nc.scalar.dma_start(out=brow_bf[2:3, :], in_=bk)
        bvb = const.tile([P, P], BF16)
        nc.scalar.dma_start(out=bvb[:], in_=bv.rearrange("o d -> (o d)").partition_broadcast(P))
        nc.scalar.activation(out=warm[:, 1:2], in_=warm[:, 0:1], func=ACT.Identity, bias=0.0, scale=1.0)

        xin = {}
        raws = {}

        def load_x(grp, parts):
            xt_in = xpool.tile([P, 4, M], BF16, name="xin")
            xin[grp] = xt_in
            b, t0 = grp // 4, 4 * (grp % 4)
            step = 4 // parts
            return [
                (xt_in[:, i * step : (i + 1) * step, :], x_view[b, :, t0 + i * step : t0 + (i + 1) * step, :])
                for i in range(parts)
            ]

        def load_table(k):
            b, t0, tn = TABLE_LOADS[k]
            rawc = const.tile([P, 3, tn, P], BF16, name="rawc%d" % k)
            nc.sync.dma_start(out=rawc[:], in_=cos_view[b, :, :, t0 : t0 + tn, :])
            rawsn = const.tile([P, 3, tn, P], BF16, name="rawsn%d" % k)
            nc.sync.dma_start(out=rawsn[:], in_=sin_view[b, :, :, t0 : t0 + tn, :])
            for i in range(tn):
                raws[(b, t0 + i)] = (rawc, rawsn, i)

        def start(pair):
            nc.sync.dma_start(out=pair[0], in_=pair[1])

        halves = [load_x(grp, 2) for grp in range(3)]
        start(halves[0][0])
        wraw = ttp.tile([P, 4096], BF16, name="tt", align_bytes=64)
        wraw_q = wraw[:, 0:2048].rearrange("p (a c) -> p a c", a=4)
        wraw_k = wraw[:, 2048:3072].rearrange("p (a c) -> p a c", a=4)
        wraw_v = wraw[:, 3072:4096].rearrange("p (a c) -> p a c", a=4)
        nc.sync.dma_start(out=wraw_q, in_=Wq.rearrange("(a p e) h d -> p a (e h d)", a=4, e=2))
        nc.sync.dma_start(out=wraw_k, in_=Wk.rearrange("(a p e) h d -> p a (e h d)", a=4, e=2))
        nc.sync.dma_start(out=wraw_v, in_=Wv.rearrange("(a p e) h d -> p a (e h d)", a=4, e=2))
        start(halves[0][1])
        load_table(0)
        start(halves[1][0])
        load_table(1)
        start(halves[1][1])
        load_table(2)
        start(halves[2][0])
        start(halves[2][1])
        for grp in (3, 4, 5):
            load_table(grp)
            start(load_x(grp, 1)[0])

        wg = ttp.tile([P, 4, 2, P, 4], BF16, name="tt", align_bytes=64)
        wc = const.tile([P, 4, 2, P], U32, align_bytes=64)
        ws = const.tile([P, 4, 2, P], U8, align_bytes=64)

        def w_source(h):
            if h < 2:
                v5 = wraw_q.rearrange("p (g u) (e c) -> p g u e c", g=2, e=2)
                return v5[:, :, :, :, h * P : (h + 1) * P]
            raw = wraw_k if h == 2 else wraw_v
            return raw.rearrange("p (g u) (e c) -> p g u e c", g=2, e=2)

        def w_regroup(h, engine):
            src5 = w_source(h)
            for g in range(2):
                dst = wg[:, h, g].rearrange("p c (u e) -> p c u e", u=2)
                src = src5[:, g].rearrange("p u e c -> p c u e")
                if engine == "scalar":
                    nc.scalar.copy(out=dst, in_=src)
                elif engine == "gpsimd":
                    nc.gpsimd.tensor_scalar(out=dst, in0=src, scalar1=1.0, scalar2=0.0, op0=ALU.mult, op1=ALU.add)
                else:
                    nc.vector.tensor_copy(out=dst, in_=src)

        def w_quantise(h):
            nc.vector.quantize_mx(
                out=wc[:, h].rearrange("p g c -> p (g c)").bitcast(FP8X4),
                scales=ws[:, h].rearrange("p g c -> p (g c)"),
                in_=wg[:, h].rearrange("p g c t -> p (g c t)"),
            )

        cs_of = {}

        def combine(k, on_vector):
            b, t0, tn = TABLE_BATCHES[k]
            rawc, rawsn, r0 = raws[(b, t0)]
            cst = const.tile([P, tn, 2, P], BF16, name="cs%d" % k)
            for i in range(tn):
                cs_of[(b, t0 + i)] = (cst, i)
            moves = [(0, raw_lo, raw_hi, rawc, comp, raw_lo) for raw_lo, raw_hi, comp in ((0, 32, 0), (32, 80, 1), (80, 128, 2))]
            moves += [(1, lo, hi, rawsn, comp, s0) for lo, hi, comp, s0 in ((0, 16, 1, 64), (16, 64, 2, 80), (64, 96, 0, 0), (96, 128, 1, 32))]
            for row, lo, hi, raw, comp, s0 in moves:
                if on_vector:
                    nc.vector.tensor_copy(out=cst[:, :, row, lo:hi], in_=raw[:, comp, r0 : r0 + tn, s0 : s0 + hi - lo])
                else:
                    nc.scalar.copy(out=cst[:, :, row, lo:hi], in_=raw[:, comp, r0 : r0 + tn, s0 : s0 + hi - lo])

        xg_of, xc_of, yt_of, yb_of, tt_of, o_of = {}, {}, {}, {}, {}, {}
        bias_col = const.tile([P, 4], F32)

        def stage_a(r):
            xt_in = xin[r // 2]
            xg = xgp.tile([P, 1024], F32, align_bytes=64)
            xg_of[r] = xg
            for j in range(2):
                words = xt_in[:, 2 * (r % 2) + j, :].bitcast(F32)
                xt = psx.tile([P, 512], F32)
                for i in range(4):
                    nc.tensor.transpose(xt[:, i * P : (i + 1) * P], words[:, i * P : (i + 1) * P], ident[:])
                    nc.tensor.transpose(xt[:, i * P : (i + 1) * P], words[:, i * P : (i + 1) * P], ident[:])
                nc.scalar.copy(
                    out=xg[:].rearrange("p (g r u) -> p g r u", g=2, u=2)[:, :, j * P : (j + 1) * P, :],
                    in_=xt[:].rearrange("p (g u r) -> p g r u", g=2, u=2),
                )

        def stage_q(r):
            xc = xcp.tile([P, 512], U32, align_bytes=64)
            xs = xcp.tile([P, 512], U8, align_bytes=64)
            xc_of[r] = (xc, xs)
            nc.vector.quantize_mx(out=xc[:].bitcast(FP8X4), scales=xs[:], in_=xg_of[r][:].bitcast(BF16))

        def stage_b(r):
            xc, xs = xc_of[r]
            m0 = psm.tile([P, 2, 256], F32)
            m1 = psm.tile([P, 256], F32)
            yt = ytp.tile([P, 3, 256], F32)
            yt_of[r] = yt
            for h in range(3):
                acc = m0[:, h, :] if h < 2 else m1[:]
                for g in range(2):
                    nc.tensor.matmul_mx(
                        out=acc,
                        lhsT=wc[:, h, g, :].bitcast(FP8X4),
                        lhsT_scale=ws[:, h, g, :],
                        rhs=xc[:, g * 256 : (g + 1) * 256].bitcast(FP8X4),
                        rhs_scale=xs[:, g * 256 : (g + 1) * 256],
                        start=(g == 0),
                        stop=(g == 1),
                    )
            for h in range(3):
                acc = m0[:, h, :] if h < 2 else m1[:]
                nc.scalar.activation(
                    out=yt[:, h, :], in_=acc, func=ACT.Identity, bias=bias_col[:, h : h + 1], scale=1.0
                )

        def stage_bv(r):
            xc, xs = xc_of[r]
            ybs = []
            for j in range(2):
                yb = psy.tile([P, 512], F32)
                ybs.append(yb)
                for g in range(2):
                    c0 = g * 256 + j * P
                    nc.tensor.matmul_mx(
                        out=yb[:, 384:512],
                        lhsT=xc[:, c0 : c0 + P].bitcast(FP8X4),
                        lhsT_scale=xs[:, c0 : c0 + P],
                        rhs=wc[:, 3, g, :].bitcast(FP8X4),
                        rhs_scale=ws[:, 3, g, :],
                        start=(g == 0),
                        stop=(g == 1),
                    )
            yb_of[r] = ybs

        def stage_dtr(r):
            yt = yt_of[r]
            for j in range(2):
                for h in range(3):
                    nc.tensor.transpose(
                        yb_of[r][j][:, h * P : (h + 1) * P], yt[:, h, j * P : (j + 1) * P], ident[:]
                    )

        def stage_e(r):
            grp = r // 2
            if r % 4 == 0:
                ov = outp.tile([P, 8, P], F32)
                oq = outp.tile([P, 8, 256], F32)
                ok = outp.tile([P, 8, P], F32)
                o_of[grp // 2] = (ov, oq, ok)
            if r % 2 == 0:
                tt = ttp.tile([P, 4, 2, 3, P], F32, align_bytes=64)
                tt_of[grp] = tt
            tt = tt_of[grp]
            ov = o_of[grp // 2][0]
            b = grp // 4
            for j in range(2):
                t4 = 2 * (r % 2) + j
                cst, ci = cs_of[(b, 4 * (grp % 4) + t4)]
                yb = yb_of[r][j]
                nc.vector.tensor_tensor(out=ov[:, 4 * (grp % 2) + t4, :], in0=yb[:, 384:512], in1=bvb[:], op=ALU.add)
                nc.vector.tensor_tensor(
                    out=tt[:, t4],
                    in0=yb[:, 0:384].rearrange("p (h d) -> p h d", h=3).unsqueeze(1).to_broadcast([P, 2, 3, P]),
                    in1=cst[:, ci].unsqueeze(2).to_broadcast([P, 2, 3, P]),
                    op=ALU.mult,
                )

        def add_q(grp, ta, tb, engine):
            tt = tt_of[grp]
            so = 4 * (grp % 2)
            oq4 = o_of[grp // 2][1][:, so : so + 4, :].rearrange("p t (h d) -> p t h d", h=2)
            engine.tensor_tensor(
                out=oq4[:, ta:tb, :, 0:64], in0=tt[:, ta:tb, 0, 0:2, 0:64], in1=tt[:, ta:tb, 1, 0:2, 64:128],
                op=ALU.subtract,
            )
            engine.tensor_tensor(
                out=oq4[:, ta:tb, :, 64:128], in0=tt[:, ta:tb, 0, 0:2, 64:128], in1=tt[:, ta:tb, 1, 0:2, 0:64],
                op=ALU.add,
            )

        def add_k(grp, ta, tb):
            tt = tt_of[grp]
            so = 4 * (grp % 2)
            ok = o_of[grp // 2][2][:, so : so + 4, :]
            nc.vector.tensor_tensor(
                out=ok[:, ta:tb, 0:64], in0=tt[:, ta:tb, 0, 2, 0:64], in1=tt[:, ta:tb, 1, 2, 64:128], op=ALU.subtract
            )
            nc.vector.tensor_tensor(
                out=ok[:, ta:tb, 64:128], in0=tt[:, ta:tb, 0, 2, 64:128], in1=tt[:, ta:tb, 1, 2, 0:64], op=ALU.add
            )

        def stores(pair, ta, tb):
            b, t0 = pair // 2, 8 * (pair % 2)
            ov, oq, ok = o_of[pair]
            nc.sync.dma_start(out=v_view[b, :, t0 + ta : t0 + tb, :], in_=ov[:, ta:tb, :])
            nc.sync.dma_start(out=q_view[b, :, t0 + ta : t0 + tb, :], in_=oq[:, ta:tb, :])
            nc.sync.dma_start(out=k_view[b, :, t0 + ta : t0 + tb, :], in_=ok[:, ta:tb, :])

        first_round = [(8 * b + t0 // 2) for b, t0, tn in TABLE_BATCHES]
        n_batches = len(TABLE_BATCHES)

        def combines(s, on_vector):
            for k in range(n_batches):
                if (k < 2) != on_vector:
                    continue
                if s == first_round[k] + (2 if k < 2 else 1):
                    combine(k, on_vector)

        for s in range(NROUND + 2):
            pending = []
            if 2 <= s <= 2:
                stage_dtr(s - 2)
            if s < NROUND:
                stage_a(s)
            if s > 2:
                stage_dtr(s - 2)
            if s == 0:
                brow_f = const.tile([P, P], F32)
                nc.vector.tensor_copy(out=brow_f[:], in_=brow_bf[:])
                bt = psm.tile([P, 256], F32, name="m1")
                nc.tensor.transpose(bt[:, 0:P], brow_f[:], ident[:])
                nc.vector.tensor_copy(out=bias_col[:], in_=bt[:, 0:4])
                w_regroup(0, "vector")
                w_regroup(1, "scalar")
                stage_q(0)
                w_regroup(2, "vector")
                w_regroup(3, "scalar")
                for h in range(4):
                    w_quantise(h)
            combines(s, True)
            if s >= 2:
                r = s - 2
                stage_e(r)
                grp = r // 2
                ta = 2 * (r % 2)
                add_q(grp, ta, ta + 2, nc.vector if r == NROUND - 1 else nc.gpsimd)
                if grp == NGROUP - 1:
                    pending.append((grp // 2, 4 + ta, 4 + ta + 2))
                elif r % 2 == 1 and grp == NGROUP - 2:
                    pending.append((grp // 2, 0, 4))
                elif r % 4 == 3:
                    pending.append((grp // 2, 0, 8))
            if 0 < s < NROUND:
                stage_q(s)
            if s >= 2:
                add_k((s - 2) // 2, 2 * (s % 2), 2 * (s % 2) + 2)
            if 1 <= s <= NROUND:
                stage_b(s - 1)
                stage_bv(s - 1)
            combines(s, False)
            if s == 3:
                load_table(6)
            if s % 2 == 1 and s // 2 + XBUFS < NGROUP:
                start(load_x(s // 2 + XBUFS, 1)[0])
            for pair, ta, tb in pending:
                stores(pair, ta, tb)
